import numpy as np
import ml_dtypes


def mxq(x, axis, fmt="e4m3"):
    dtype, down = {"e4m3": (ml_dtypes.float8_e4m3fn, 7), "e5m2": (ml_dtypes.float8_e5m2, 14)}[fmt]
    v = np.moveaxis(np.asarray(x, np.float32).astype(ml_dtypes.bfloat16).astype(np.float64), axis, -1)
    blocks = v.reshape(v.shape[:-1] + (-1, 32))
    amax = np.abs(blocks).max(-1, keepdims=True)
    byte = np.maximum(np.where(amax > 0, np.frexp(amax)[1] - 1 + 127, 0) - down, 1)
    scale = np.exp2(byte - 127.0)
    codes = (blocks / scale).astype(np.float32).astype(dtype).astype(np.float64)
    return np.moveaxis((codes * scale).reshape(v.shape), -1, axis)


WIDE = False


def mx_kscale(k):
    if not WIDE:
        return np.ones(k)
    levels = np.array([10, -10, 5, -5, 0])
    a = np.random.permutation(np.resize(levels, k // 512 * 4)).reshape(k // 512, 4)
    idx = np.arange(k)
    return np.exp2(a[idx // 512, idx % 128 // 32])


BF16 = ml_dtypes.bfloat16


def bf(x):
    return np.asarray(x, np.float32).astype(BF16)


def f64(x):
    return np.asarray(x).astype(np.float64)


B, N, E, H, G, C, EO = 1, 2048, 1024, 8, 128, 512, 1024
LN_EPS = 1e-5


def sigmoid(v):
    return 1.0 / (1.0 + np.exp(-v))


def layernorm(y, w, b):
    mu = y.mean(-1, keepdims=True)
    var = np.square(y - mu).mean(-1, keepdims=True)
    return (y - mu) / np.sqrt(var + LN_EPS) * w + b


def setup_inputs():
    s = mx_kscale(E)
    return {"attn": bf((1.5 + 2.5 * np.random.standard_normal((B, N, E))) * s),
            "gate_low": bf(np.random.standard_normal((B, N, G))),
            "Wg2": bf(np.random.standard_normal((G, E)) / np.sqrt(G)),
            "Wo": bf(np.random.standard_normal((E, EO)) / np.sqrt(E) / s[:, None]),
            "ln_w": bf(1.0 + 0.1 * np.random.standard_normal(EO)),
            "ln_b": bf(0.1 * np.random.standard_normal(EO))}


def reference(attn, gate_low, Wg2, Wo, ln_w, ln_b):
    gate = sigmoid(f64(gate_low) @ f64(Wg2))
    h = f64(attn) * gate
    y = mxq(h, 2, "e4m3") @ mxq(f64(Wo), 0, "e4m3")
    return layernorm(y, f64(ln_w), f64(ln_b))

@@ -1,0 +1,285 @@
+from contextlib import ExitStack
+
+import concourse.mybir as mybir
+from concourse.masks import make_identity
+
+F32 = mybir.dt.float32
+BF16 = mybir.dt.bfloat16
+U32 = mybir.dt.uint32
+U8 = mybir.dt.uint8
+FP8X4 = mybir.dt.float8_e4m3fn_x4
+ACT = mybir.ActivationFunctionType
+ALU = mybir.AluOpType
+
+P = 128
+TOKENS = 2048
+E = 1024
+D_GATE = 128
+E_OUT = 1024
+LN_EPS = 1e-5
+
+TILES = TOKENS // P
+PAIRS = TILES // 2
+PAIR_TOKENS = 2 * P
+PACK = 4
+PASSES = E // (P * PACK)
+BANK = 512
+HALVES = E_OUT // BANK
+WO_CHUNK = 256
+WO_CHUNKS_PER_PASS = E_OUT // WO_CHUNK
+
+FLOPS = 2 * TOKENS * E * E_OUT + 2 * TOKENS * D_GATE * E
+
+
+def tile_tnlattention_pb_kernel(tc, attn, gate_low, Wg2, Wo, ln_w, ln_b, out):
+    nc = tc.nc
+    attn_rows = attn.flatten_outer_dims().rearrange("(p i) e -> p (i e)", i=TILES)
+    gate_low_rows = gate_low.flatten_outer_dims().rearrange("(p i) d -> p (i d)", i=TILES)
+    out_rows = out.flatten_outer_dims().rearrange("(p i) n -> p (i n)", i=TILES)
+
+    with ExitStack() as pools:
+        keep = pools.enter_context(tc.tile_pool(name="keep", bufs=1))
+        attn_pool = pools.enter_context(tc.tile_pool(name="attn", bufs=PAIRS))
+        stage1 = pools.enter_context(tc.tile_pool(name="stage1", bufs=3))
+        stage2 = pools.enter_context(tc.tile_pool(name="stage2", bufs=4))
+        psum = pools.enter_context(tc.psum_pool(name="psum", bufs=8))
+
+        gate_low_sb = keep.tile([P, TILES * D_GATE], BF16)
+        nc.sync.dma_start(out=gate_low_sb[:], in_=gate_low_rows)
+        wg2_sb = keep.tile([P, E], BF16)
+        nc.sync.dma_start(out=wg2_sb[:], in_=Wg2)
+
+        wo_raw = keep.tile([P, PASSES, PACK, E_OUT], BF16)
+        attn_sb = []
+        for pair in range(PAIRS):
+            attn_pair = attn_pool.tile([P, 2 * E], BF16)
+            nc.sync.dma_start(
+                out=attn_pair[:], in_=attn_rows[:, pair * 2 * E : (pair + 1) * 2 * E]
+            )
+            attn_sb.append(attn_pair)
+            if 1 <= pair <= PASSES:
+                g = pair - 1
+                nc.sync.dma_start(
+                    out=wo_raw[:, g].rearrange("p (u e) n -> p u e n", e=2),
+                    in_=Wo[g * P * PACK : (g + 1) * P * PACK, :].rearrange(
+                        "(u p e) n -> p u e n", u=2, e=2
+                    ),
+                )
+        ln_w_rows = keep.tile([P, E_OUT], BF16)
+        nc.sync.dma_start(out=ln_w_rows[:], in_=ln_w.partition_broadcast(P))
+        ln_b_rows = keep.tile([P, E_OUT], BF16)
+        nc.sync.dma_start(out=ln_b_rows[:], in_=ln_b.partition_broadcast(P))
+
+        ident_bf16 = keep.tile([P, P], BF16)
+        make_identity(nc, ident_bf16[:])
+        ident_f32 = keep.tile([P, P], F32)
+        make_identity(nc, ident_f32[:])
+        minus_half = keep.tile([P, 1], F32)
+        nc.gpsimd.memset(minus_half[:], -0.5)
+
+        table_in = keep.tile([P, 1], F32)
+        nc.vector.memset(table_in[:], 0.0)
+        table_out = keep.tile([P, 1], F32)
+        nc.scalar.activation(out=table_out[:], in_=table_in[:], func=ACT.Sigmoid)
+
+        wg2_words = keep.tile([P, PASSES * 2, 2, P], BF16)
+        nc.vector.tensor_copy(
+            out=wg2_words[:],
+            in_=wg2_sb[:].rearrange("d (a p e) -> d a e p", a=PASSES * 2, e=2),
+        )
+
+        gate_lowT = keep.tile([P, TILES * P], BF16)
+        tiles_per_bank = 2 * BANK // P
+        for first in range(0, TILES, tiles_per_bank):
+            turned = psum.tile([P, tiles_per_bank * P], BF16, tag="bank")
+            for j in range(tiles_per_bank):
+                i = first + j
+                nc.tensor.transpose(
+                    out=turned[:, j * P : (j + 1) * P],
+                    in_=gate_low_sb[:, i * D_GATE : (i + 1) * D_GATE],
+                    identity=ident_bf16[:],
+                )
+            nc.vector.tensor_copy(
+                out=gate_lowT[:, first * P : (first + tiles_per_bank) * P], in_=turned[:]
+            )
+
+        wo_grouped = keep.tile([P, PASSES, E_OUT, PACK], BF16, align_bytes=64)
+        wo_codes = keep.tile([P, PASSES, E_OUT], U32, align_bytes=64)
+        wo_scales = keep.tile([P, PASSES, E_OUT], U8, align_bytes=64)
+        h_codes = keep.tile([P, PAIRS, PASSES, PAIR_TOKENS], U32, align_bytes=64)
+        h_scales = keep.tile([P, PAIRS, PASSES, PAIR_TOKENS], U8, align_bytes=64)
+
+        def regroup_wo(chunk):
+            g, quarter = divmod(chunk, WO_CHUNKS_PER_PASS)
+            cols = slice(quarter * WO_CHUNK, (quarter + 1) * WO_CHUNK)
+            nc.scalar.copy(
+                out=wo_grouped[:, g, cols, :],
+                in_=wo_raw[:, g, :, cols].rearrange("p t n -> p n t"),
+            )
+
+        def quantise_wo(g):
+            nc.vector.quantize_mx(
+                out=wo_codes[:, g, :].bitcast(FP8X4),
+                scales=wo_scales[:, g, :],
+                in_=wo_grouped[:, g].rearrange("p n t -> p (n t)"),
+            )
+
+        def gated_unit(pair, g, h_grouped):
+            attn_words = attn_sb[pair][:].bitcast(F32)
+            attnT = psum.tile([P, BANK], F32, tag="bank")
+            for u in range(2):
+                for half in range(2):
+                    word0 = half * (E // 2) + (2 * g + u) * P
+                    nc.tensor.transpose(
+                        out=attnT[:, (2 * u + half) * P : (2 * u + half + 1) * P],
+                        in_=attn_words[:, word0 : word0 + P],
+                        identity=ident_f32[:],
+                    )
+            sig = stage1.tile([P, PAIR_TOKENS, PACK], F32)
+            for half in range(2):
+                i = 2 * pair + half
+                gateT = psum.tile([P, PACK, P], F32, tag="bank")
+                for t in range(PACK):
+                    u, e = divmod(t, 2)
+                    nc.tensor.matmul(
+                        out=gateT[:, t, :],
+                        lhsT=wg2_words[:, 2 * g + u, e, :],
+                        rhs=gate_lowT[:, i * P : (i + 1) * P],
+                        start=True,
+                        stop=True,
+                    )
+                nc.scalar.activation(
+                    out=sig[:, half * P : (half + 1) * P, :],
+                    in_=gateT[:].rearrange("p t m -> p m t"),
+                    func=ACT.Sigmoid,
+                )
+            nc.vector.tensor_tensor(
+                out=h_grouped[:, g].rearrange("p m (u e) -> p m u e", e=2),
+                in0=attnT[:].bitcast(BF16).rearrange("p (u m e) -> p m u e", u=2, e=2),
+                in1=sig[:].rearrange("p m (u e) -> p m u e", e=2),
+                op=ALU.mult,
+            )
+
+        def quantise_h(pair, h_grouped):
+            nc.vector.quantize_mx(
+                out=h_codes[:, pair].rearrange("p g m -> p (g m)").bitcast(FP8X4),
+                scales=h_scales[:, pair].rearrange("p g m -> p (g m)"),
+                in_=h_grouped[:].rearrange("p g m t -> p (g m t)"),
+            )
+
+        h_grouped_of = {}
+        for unit in range(PAIRS * PASSES):
+            pair, g = divmod(unit, PASSES)
+            if g == 0:
+                h_grouped = stage1.tile([P, PASSES, PAIR_TOKENS, PACK], BF16, align_bytes=64)
+                h_grouped_of[pair] = h_grouped
+            gated_unit(pair, g, h_grouped_of[pair])
+            if unit < PASSES * WO_CHUNKS_PER_PASS:
+                regroup_wo(unit)
+                if unit % WO_CHUNKS_PER_PASS == WO_CHUNKS_PER_PASS - 1:
+                    quantise_wo(unit // WO_CHUNKS_PER_PASS)
+            if g == 0 and pair >= 1:
+                quantise_h(pair - 1, h_grouped_of[pair - 1])
+        quantise_h(PAIRS - 1, h_grouped_of[PAIRS - 1])
+
+        y_of = {}
+        y_copy_of = {}
+        neg_mean_of = {}
+        rstd_of = {}
+
+        def project(i):
+            pair, half = divmod(i, 2)
+            tokens = slice(half * P, (half + 1) * P)
+            banks = []
+            for n_half in range(HALVES):
+                cols = slice(n_half * BANK, (n_half + 1) * BANK)
+                y = psum.tile([P, BANK], F32, tag="bank")
+                for g in range(PASSES):
+                    nc.tensor.matmul_mx(
+                        out=y[:],
+                        lhsT=h_codes[:, pair, g, tokens].bitcast(FP8X4),
+                        lhsT_scale=h_scales[:, pair, g, tokens],
+                        rhs=wo_codes[:, g, cols].bitcast(FP8X4),
+                        rhs_scale=wo_scales[:, g, cols],
+                        start=(g == 0),
+                        stop=(g == PASSES - 1),
+                    )
+                banks.append(y)
+            y_of[i] = banks
+
+        def row_means(i):
+            y_copy = stage2.tile([P, E_OUT], F32)
+            sums = stage2.tile([P, HALVES], F32)
+            for n_half in range(HALVES):
+                nc.scalar.activation(
+                    out=y_copy[:, n_half * BANK : (n_half + 1) * BANK],
+                    in_=y_of[i][n_half][:],
+                    func=ACT.Identity,
+                    accum_out=sums[:, n_half : n_half + 1],
+                )
+            neg_mean = stage2.tile([P, 1], F32)
+            nc.gpsimd.tensor_scalar(
+                out=neg_mean[:],
+                in0=sums[:, 0:1],
+                scalar1=sums[:, 1:2],
+                scalar2=-1.0 / E_OUT,
+                op0=ALU.add,
+                op1=ALU.mult,
+            )
+            y_copy_of[i] = y_copy
+            neg_mean_of[i] = neg_mean
+
+        def row_rstds(i):
+            squares = stage2.tile([P, E_OUT], BF16)
+            square_sum = stage2.tile([P, 1], F32)
+            nc.scalar.activation(
+                out=squares[:],
+                in_=y_copy_of[i][:],
+                func=ACT.Square,
+                bias=neg_mean_of[i][:, 0:1],
+                accum_out=square_sum[:],
+            )
+            var_eps = stage2.tile([P, 1], F32)
+            nc.gpsimd.tensor_scalar(
+                out=var_eps[:],
+                in0=square_sum[:],
+                scalar1=1.0 / E_OUT,
+                scalar2=LN_EPS,
+                op0=ALU.mult,
+                op1=ALU.add,
+            )
+            rstd = stage2.tile([P, 1], F32)
+            nc.gpsimd.tensor_tensor(out=rstd[:], in0=var_eps[:], in1=minus_half[:], op=ALU.pow)
+            rstd_of[i] = rstd
+
+        def normalise(i):
+            centred = stage2.tile([P, E_OUT], F32)
+            for n_half in range(HALVES):
+                cols = slice(n_half * BANK, (n_half + 1) * BANK)
+                nc.vector.scalar_tensor_tensor(
+                    out=centred[:, cols],
+                    in0=y_of[i][n_half][:],
+                    scalar=neg_mean_of[i][:, 0:1],
+                    in1=ln_w_rows[:, cols],
+                    op0=ALU.add,
+                    op1=ALU.mult,
+                )
+            result = stage2.tile([P, E_OUT], F32)
+            nc.vector.scalar_tensor_tensor(
+                out=result[:],
+                in0=centred[:],
+                scalar=rstd_of[i][:, 0:1],
+                in1=ln_b_rows[:],
+                op0=ALU.mult,
+                op1=ALU.add,
+            )
+            nc.sync.dma_start(out=out_rows[:, i * E_OUT : (i + 1) * E_OUT], in_=result[:])
+
+        for step in range(TILES + 2):
+            if step < TILES:
+                project(step)
+                row_means(step)
+            if 1 <= step <= TILES:
+                row_rstds(step - 1)
+            if step >= 2:
+                normalise(step - 2)

@@ -23,10 +23,13 @@ PAIRS = TILES // 2
 PAIR_TOKENS = 2 * P
 PACK = 4
 PASSES = E // (P * PACK)
+UNITS = PAIRS * PASSES
 BANK = 512
 HALVES = E_OUT // BANK
-WO_CHUNK = 256
+WO_CHUNK = 128
 WO_CHUNKS_PER_PASS = E_OUT // WO_CHUNK
+WO_CHUNKS = PASSES * WO_CHUNKS_PER_PASS
+WO_FIRST_UNIT = 2
 
 FLOPS = 2 * TOKENS * E * E_OUT + 2 * TOKENS * D_GATE * E
 
@@ -37,26 +40,24 @@ def tile_tnlattention_pb_kernel(tc, attn, gate_low, Wg2, Wo, ln_w, ln_b, out):
     gate_low_rows = gate_low.flatten_outer_dims().rearrange("(p i) d -> p (i d)", i=TILES)
     out_rows = out.flatten_outer_dims().rearrange("(p i) n -> p (i n)", i=TILES)
 
-    with ExitStack() as pools:
-        keep = pools.enter_context(tc.tile_pool(name="keep", bufs=1))
-        attn_pool = pools.enter_context(tc.tile_pool(name="attn", bufs=PAIRS))
-        stage1 = pools.enter_context(tc.tile_pool(name="stage1", bufs=3))
-        stage2 = pools.enter_context(tc.tile_pool(name="stage2", bufs=4))
-        psum = pools.enter_context(tc.psum_pool(name="psum", bufs=8))
+    with ExitStack() as stack:
+        keep = stack.enter_context(tc.tile_pool(name="keep", bufs=1))
+        stage1 = stack.enter_context(tc.tile_pool(name="stage1", bufs=3))
+        stage2 = stack.enter_context(tc.tile_pool(name="stage2", bufs=4))
+        psum_keep = stack.enter_context(tc.psum_pool(name="psum_keep", bufs=1))
+        psum = stack.enter_context(tc.psum_pool(name="psum", bufs=6))
 
-        gate_low_sb = keep.tile([P, TILES * D_GATE], BF16)
-        nc.sync.dma_start(out=gate_low_sb[:], in_=gate_low_rows)
         wg2_sb = keep.tile([P, E], BF16)
-        nc.sync.dma_start(out=wg2_sb[:], in_=Wg2)
-
+        gate_low_sb = keep.tile([P, TILES * D_GATE], BF16)
+        attn_sb = keep.tile([P, TILES * E], BF16)
         wo_raw = keep.tile([P, PASSES, PACK, E_OUT], BF16)
-        attn_sb = []
         for pair in range(PAIRS):
-            attn_pair = attn_pool.tile([P, 2 * E], BF16)
-            nc.sync.dma_start(
-                out=attn_pair[:], in_=attn_rows[:, pair * 2 * E : (pair + 1) * 2 * E]
-            )
-            attn_sb.append(attn_pair)
+            gate_cols = slice(pair * 2 * D_GATE, (pair + 1) * 2 * D_GATE)
+            nc.sync.dma_start(out=gate_low_sb[:, gate_cols], in_=gate_low_rows[:, gate_cols])
+            if pair == 0:
+                nc.sync.dma_start(out=wg2_sb[:], in_=Wg2)
+            attn_cols = slice(pair * 2 * E, (pair + 1) * 2 * E)
+            nc.sync.dma_start(out=attn_sb[:, attn_cols], in_=attn_rows[:, attn_cols])
             if 1 <= pair <= PASSES:
                 g = pair - 1
                 nc.sync.dma_start(
@@ -82,59 +83,48 @@ def tile_tnlattention_pb_kernel(tc, attn, gate_low, Wg2, Wo, ln_w, ln_b, out):
         table_out = keep.tile([P, 1], F32)
         nc.scalar.activation(out=table_out[:], in_=table_in[:], func=ACT.Sigmoid)
 
-        wg2_words = keep.tile([P, PASSES * 2, 2, P], BF16)
-        nc.vector.tensor_copy(
-            out=wg2_words[:],
-            in_=wg2_sb[:].rearrange("d (a p e) -> d a e p", a=PASSES * 2, e=2),
-        )
-
-        gate_lowT = keep.tile([P, TILES * P], BF16)
-        tiles_per_bank = 2 * BANK // P
-        for first in range(0, TILES, tiles_per_bank):
-            turned = psum.tile([P, tiles_per_bank * P], BF16, tag="bank")
-            for j in range(tiles_per_bank):
-                i = first + j
-                nc.tensor.transpose(
-                    out=turned[:, j * P : (j + 1) * P],
-                    in_=gate_low_sb[:, i * D_GATE : (i + 1) * D_GATE],
-                    identity=ident_bf16[:],
-                )
-            nc.vector.tensor_copy(
-                out=gate_lowT[:, first * P : (first + tiles_per_bank) * P], in_=turned[:]
-            )
+        wg2_by_word = wg2_sb[:].rearrange("d (a p e) -> d a e p", a=PASSES * 2, e=2)
+        attn_words = attn_sb[:].bitcast(F32)
 
         wo_grouped = keep.tile([P, PASSES, E_OUT, PACK], BF16, align_bytes=64)
         wo_codes = keep.tile([P, PASSES, E_OUT], U32, align_bytes=64)
         wo_scales = keep.tile([P, PASSES, E_OUT], U8, align_bytes=64)
         h_codes = keep.tile([P, PAIRS, PASSES, PAIR_TOKENS], U32, align_bytes=64)
         h_scales = keep.tile([P, PAIRS, PASSES, PAIR_TOKENS], U8, align_bytes=64)
+        gate_lowT = keep.tile([P, TILES * P], BF16)
+
+        def wo_chunk(chunk):
+            g, quarter = divmod(chunk, WO_CHUNKS_PER_PASS)
+            return g, slice(quarter * WO_CHUNK, (quarter + 1) * WO_CHUNK)
 
         def regroup_wo(chunk):
-            g, quarter = divmod(chunk, WO_CHUNKS_PER_PASS)
-            cols = slice(quarter * WO_CHUNK, (quarter + 1) * WO_CHUNK)
-            nc.scalar.copy(
-                out=wo_grouped[:, g, cols, :],
-                in_=wo_raw[:, g, :, cols].rearrange("p t n -> p n t"),
+            g, cols = wo_chunk(chunk)
+            grouped = wo_grouped[:, g, cols, :].rearrange("p (c i) t -> p c t i", i=4)
+            raw = wo_raw[:, g, :, cols].rearrange("p t (c i) -> p c t i", i=4)
+            nc.scalar.copy(out=grouped, in_=raw)
+
+        def quantise_wo(chunk):
+            g, cols = wo_chunk(chunk)
+            nc.vector.quantize_mx(
+                out=wo_codes[:, g, cols].bitcast(FP8X4),
+                scales=wo_scales[:, g, cols],
+                in_=wo_grouped[:, g, cols, :].rearrange("p n t -> p (n t)"),
             )
 
-        def quantise_wo(g):
-            nc.vector.quantize_mx(
-                out=wo_codes[:, g, :].bitcast(FP8X4),
-                scales=wo_scales[:, g, :],
-                in_=wo_grouped[:, g].rearrange("p n t -> p (n t)"),
+        def turn_gate_low(pair):
+            turned = psum.tile([P, PAIR_TOKENS], BF16, tag="bank")
+            for half in range(2):
+                i = 2 * pair + half
+                nc.tensor.transpose(
+                    out=turned[:, half * P : (half + 1) * P],
+                    in_=gate_low_sb[:, i * D_GATE : (i + 1) * D_GATE],
+                    identity=ident_bf16[:],
+                )
+            nc.vector.tensor_copy(
+                out=gate_lowT[:, pair * PAIR_TOKENS : (pair + 1) * PAIR_TOKENS], in_=turned[:]
             )
 
         def gated_unit(pair, g, h_grouped):
-            attn_words = attn_sb[pair][:].bitcast(F32)
-            attnT = psum.tile([P, BANK], F32, tag="bank")
-            for u in range(2):
-                for half in range(2):
-                    word0 = half * (E // 2) + (2 * g + u) * P
-                    nc.tensor.transpose(
-                        out=attnT[:, (2 * u + half) * P : (2 * u + half + 1) * P],
-                        in_=attn_words[:, word0 : word0 + P],
-                        identity=ident_f32[:],
-                    )
             sig = stage1.tile([P, PAIR_TOKENS, PACK], F32)
             for half in range(2):
                 i = 2 * pair + half
@@ -143,7 +133,7 @@ def tile_tnlattention_pb_kernel(tc, attn, gate_low, Wg2, Wo, ln_w, ln_b, out):
                     u, e = divmod(t, 2)
                     nc.tensor.matmul(
                         out=gateT[:, t, :],
-                        lhsT=wg2_words[:, 2 * g + u, e, :],
+                        lhsT=wg2_by_word[:, 2 * g + u, e, :],
                         rhs=gate_lowT[:, i * P : (i + 1) * P],
                         start=True,
                         stop=True,
@@ -153,6 +143,15 @@ def tile_tnlattention_pb_kernel(tc, attn, gate_low, Wg2, Wo, ln_w, ln_b, out):
                     in_=gateT[:].rearrange("p t m -> p m t"),
                     func=ACT.Sigmoid,
                 )
+            attnT = psum.tile([P, BANK], F32, tag="bank")
+            for u in range(2):
+                for half in range(2):
+                    word0 = (2 * pair + half) * (E // 2) + (2 * g + u) * P
+                    nc.tensor.transpose(
+                        out=attnT[:, (2 * u + half) * P : (2 * u + half + 1) * P],
+                        in_=attn_words[:, word0 : word0 + P],
+                        identity=ident_f32[:],
+                    )
             nc.vector.tensor_tensor(
                 out=h_grouped[:, g].rearrange("p m (u e) -> p m u e", e=2),
                 in0=attnT[:].bitcast(BF16).rearrange("p (u m e) -> p m u e", u=2, e=2),
@@ -168,24 +167,29 @@ def tile_tnlattention_pb_kernel(tc, attn, gate_low, Wg2, Wo, ln_w, ln_b, out):
             )
 
         h_grouped_of = {}
-        for unit in range(PAIRS * PASSES):
-            pair, g = divmod(unit, PASSES)
-            if g == 0:
-                h_grouped = stage1.tile([P, PASSES, PAIR_TOKENS, PACK], BF16, align_bytes=64)
-                h_grouped_of[pair] = h_grouped
-            gated_unit(pair, g, h_grouped_of[pair])
-            if unit < PASSES * WO_CHUNKS_PER_PASS:
-                regroup_wo(unit)
-                if unit % WO_CHUNKS_PER_PASS == WO_CHUNKS_PER_PASS - 1:
-                    quantise_wo(unit // WO_CHUNKS_PER_PASS)
-            if g == 0 and pair >= 1:
+        turn_gate_low(0)
+        for step in range(UNITS + WO_FIRST_UNIT + 1):
+            pair, g = divmod(step, PASSES)
+            if step < UNITS:
+                if g == 0:
+                    h_grouped = stage1.tile([P, PASSES, PAIR_TOKENS, PACK], BF16, align_bytes=64)
+                    h_grouped_of[pair] = h_grouped
+                if g == PASSES - 1 and pair + 1 < PAIRS:
+                    turn_gate_low(pair + 1)
+                gated_unit(pair, g, h_grouped_of[pair])
+            chunk = step - WO_FIRST_UNIT
+            if 0 <= chunk < WO_CHUNKS:
+                regroup_wo(chunk)
+            if 0 <= chunk - 1 < WO_CHUNKS:
+                quantise_wo(chunk - 1)
+            if g == 0 and 1 <= pair <= PAIRS:
                 quantise_h(pair - 1, h_grouped_of[pair - 1])
-        quantise_h(PAIRS - 1, h_grouped_of[PAIRS - 1])
 
         y_of = {}
         y_copy_of = {}
         neg_mean_of = {}
         rstd_of = {}
+        centred_of = {}
 
         def project(i):
             pair, half = divmod(i, 2)
@@ -252,7 +256,7 @@ def tile_tnlattention_pb_kernel(tc, attn, gate_low, Wg2, Wo, ln_w, ln_b, out):
             nc.gpsimd.tensor_tensor(out=rstd[:], in0=var_eps[:], in1=minus_half[:], op=ALU.pow)
             rstd_of[i] = rstd
 
-        def normalise(i):
+        def centre(i):
             centred = stage2.tile([P, E_OUT], F32)
             for n_half in range(HALVES):
                 cols = slice(n_half * BANK, (n_half + 1) * BANK)
@@ -264,16 +268,36 @@ def tile_tnlattention_pb_kernel(tc, attn, gate_low, Wg2, Wo, ln_w, ln_b, out):
                     op0=ALU.add,
                     op1=ALU.mult,
                 )
-            result = stage2.tile([P, E_OUT], F32)
-            nc.vector.scalar_tensor_tensor(
-                out=result[:],
-                in0=centred[:],
-                scalar=rstd_of[i][:, 0:1],
-                in1=ln_b_rows[:],
-                op0=ALU.mult,
-                op1=ALU.add,
+            centred_of[i] = centred
+
+        ln_b_banks = []
+        for n_half in range(HALVES):
+            ln_b_bank = psum_keep.tile([P, BANK], F32, name="ln_b_bank%d" % n_half)
+            nc.tensor.matmul(
+                out=ln_b_bank[:],
+                lhsT=ident_bf16[:],
+                rhs=ln_b_rows[:, n_half * BANK : (n_half + 1) * BANK],
+                start=True,
+                stop=True,
             )
-            nc.sync.dma_start(out=out_rows[:, i * E_OUT : (i + 1) * E_OUT], in_=result[:])
+            ln_b_banks.append(ln_b_bank)
+
+        def scale_and_store(i):
+            result = stage2.tile([P, E_OUT], F32)
+            for n_half in range(HALVES):
+                cols = slice(n_half * BANK, (n_half + 1) * BANK)
+                nc.vector.scalar_tensor_tensor(
+                    out=result[:, cols],
+                    in0=centred_of[i][:, cols],
+                    scalar=rstd_of[i][:, 0:1],
+                    in1=ln_b_banks[n_half][:],
+                    op0=ALU.mult,
+                    op1=ALU.add,
+                )
+                nc.sync.dma_start(
+                    out=out_rows[:, i * E_OUT + n_half * BANK : i * E_OUT + (n_half + 1) * BANK],
+                    in_=result[:, cols],
+                )
 
         for step in range(TILES + 2):
             if step < TILES:
@@ -281,5 +305,6 @@ def tile_tnlattention_pb_kernel(tc, attn, gate_low, Wg2, Wo, ln_w, ln_b, out):
                 row_means(step)
             if 1 <= step <= TILES:
                 row_rstds(step - 1)
+                centre(step - 1)
             if step >= 2:
-                normalise(step - 2)
+                scale_and_store(step - 2)

@@ -26,7 +26,7 @@ PASSES = E // (P * PACK)
 UNITS = PAIRS * PASSES
 BANK = 512
 HALVES = E_OUT // BANK
-WO_CHUNK = 128
+WO_CHUNK = 256
 WO_CHUNKS_PER_PASS = E_OUT // WO_CHUNK
 WO_CHUNKS = PASSES * WO_CHUNKS_PER_PASS
 WO_FIRST_UNIT = 2
@@ -99,16 +99,20 @@ def tile_tnlattention_pb_kernel(tc, attn, gate_low, Wg2, Wo, ln_w, ln_b, out):
 
         def regroup_wo(chunk):
             g, cols = wo_chunk(chunk)
-            grouped = wo_grouped[:, g, cols, :].rearrange("p (c i) t -> p c t i", i=4)
-            raw = wo_raw[:, g, :, cols].rearrange("p t (c i) -> p c t i", i=4)
-            nc.scalar.copy(out=grouped, in_=raw)
+            nc.gpsimd.tensor_scalar(
+                out=wo_grouped[:, g, cols, :],
+                in0=wo_raw[:, g, :, cols].rearrange("p t n -> p n t"),
+                scalar1=1.0,
+                scalar2=0.0,
+                op0=ALU.mult,
+                op1=ALU.add,
+            )
 
-        def quantise_wo(chunk):
-            g, cols = wo_chunk(chunk)
+        def quantise_wo(g):
             nc.vector.quantize_mx(
-                out=wo_codes[:, g, cols].bitcast(FP8X4),
-                scales=wo_scales[:, g, cols],
-                in_=wo_grouped[:, g, cols, :].rearrange("p n t -> p (n t)"),
+                out=wo_codes[:, g, :].bitcast(FP8X4),
+                scales=wo_scales[:, g, :],
+                in_=wo_grouped[:, g].rearrange("p n t -> p (n t)"),
             )
 
         def turn_gate_low(pair):
@@ -120,7 +124,7 @@ def tile_tnlattention_pb_kernel(tc, attn, gate_low, Wg2, Wo, ln_w, ln_b, out):
                     in_=gate_low_sb[:, i * D_GATE : (i + 1) * D_GATE],
                     identity=ident_bf16[:],
                 )
-            nc.vector.tensor_copy(
+            nc.scalar.copy(
                 out=gate_lowT[:, pair * PAIR_TOKENS : (pair + 1) * PAIR_TOKENS], in_=turned[:]
             )
 
@@ -180,8 +184,8 @@ def tile_tnlattention_pb_kernel(tc, attn, gate_low, Wg2, Wo, ln_w, ln_b, out):
             chunk = step - WO_FIRST_UNIT
             if 0 <= chunk < WO_CHUNKS:
                 regroup_wo(chunk)
-            if 0 <= chunk - 1 < WO_CHUNKS:
-                quantise_wo(chunk - 1)
+            if chunk >= 2 and (chunk - 1) % WO_CHUNKS_PER_PASS == 0 and (chunk - 1) // WO_CHUNKS_PER_PASS <= PASSES:
+                quantise_wo((chunk - 1) // WO_CHUNKS_PER_PASS - 1)
             if g == 0 and 1 <= pair <= PAIRS:
                 quantise_h(pair - 1, h_grouped_of[pair - 1])
 

@@ -26,7 +26,7 @@ PASSES = E // (P * PACK)
 UNITS = PAIRS * PASSES
 BANK = 512
 HALVES = E_OUT // BANK
-WO_CHUNK = 256
+WO_CHUNK = 128
 WO_CHUNKS_PER_PASS = E_OUT // WO_CHUNK
 WO_CHUNKS = PASSES * WO_CHUNKS_PER_PASS
 WO_FIRST_UNIT = 2
@@ -44,7 +44,6 @@ def tile_tnlattention_pb_kernel(tc, attn, gate_low, Wg2, Wo, ln_w, ln_b, out):
         keep = stack.enter_context(tc.tile_pool(name="keep", bufs=1))
         stage1 = stack.enter_context(tc.tile_pool(name="stage1", bufs=3))
         stage2 = stack.enter_context(tc.tile_pool(name="stage2", bufs=4))
-        psum_keep = stack.enter_context(tc.psum_pool(name="psum_keep", bufs=1))
         psum = stack.enter_context(tc.psum_pool(name="psum", bufs=6))
 
         wg2_sb = keep.tile([P, E], BF16)
@@ -99,20 +98,16 @@ def tile_tnlattention_pb_kernel(tc, attn, gate_low, Wg2, Wo, ln_w, ln_b, out):
 
         def regroup_wo(chunk):
             g, cols = wo_chunk(chunk)
-            nc.gpsimd.tensor_scalar(
-                out=wo_grouped[:, g, cols, :],
-                in0=wo_raw[:, g, :, cols].rearrange("p t n -> p n t"),
-                scalar1=1.0,
-                scalar2=0.0,
-                op0=ALU.mult,
-                op1=ALU.add,
-            )
+            grouped = wo_grouped[:, g, cols, :].rearrange("p (c i) t -> p c t i", i=4)
+            raw = wo_raw[:, g, :, cols].rearrange("p t (c i) -> p c t i", i=4)
+            nc.scalar.copy(out=grouped, in_=raw)
 
-        def quantise_wo(g):
+        def quantise_wo(chunk):
+            g, cols = wo_chunk(chunk)
             nc.vector.quantize_mx(
-                out=wo_codes[:, g, :].bitcast(FP8X4),
-                scales=wo_scales[:, g, :],
-                in_=wo_grouped[:, g].rearrange("p n t -> p (n t)"),
+                out=wo_codes[:, g, cols].bitcast(FP8X4),
+                scales=wo_scales[:, g, cols],
+                in_=wo_grouped[:, g, cols, :].rearrange("p n t -> p (n t)"),
             )
 
         def turn_gate_low(pair):
@@ -124,7 +119,7 @@ def tile_tnlattention_pb_kernel(tc, attn, gate_low, Wg2, Wo, ln_w, ln_b, out):
                     in_=gate_low_sb[:, i * D_GATE : (i + 1) * D_GATE],
                     identity=ident_bf16[:],
                 )
-            nc.scalar.copy(
+            nc.vector.tensor_copy(
                 out=gate_lowT[:, pair * PAIR_TOKENS : (pair + 1) * PAIR_TOKENS], in_=turned[:]
             )
 
@@ -184,8 +179,8 @@ def tile_tnlattention_pb_kernel(tc, attn, gate_low, Wg2, Wo, ln_w, ln_b, out):
             chunk = step - WO_FIRST_UNIT
             if 0 <= chunk < WO_CHUNKS:
                 regroup_wo(chunk)
-            if chunk >= 2 and (chunk - 1) % WO_CHUNKS_PER_PASS == 0 and (chunk - 1) // WO_CHUNKS_PER_PASS <= PASSES:
-                quantise_wo((chunk - 1) // WO_CHUNKS_PER_PASS - 1)
+            if 0 <= chunk - 1 < WO_CHUNKS:
+                quantise_wo(chunk - 1)
             if g == 0 and 1 <= pair <= PAIRS:
                 quantise_h(pair - 1, h_grouped_of[pair - 1])
 
@@ -274,18 +269,6 @@ def tile_tnlattention_pb_kernel(tc, attn, gate_low, Wg2, Wo, ln_w, ln_b, out):
                 )
             centred_of[i] = centred
 
-        ln_b_banks = []
-        for n_half in range(HALVES):
-            ln_b_bank = psum_keep.tile([P, BANK], F32, name="ln_b_bank%d" % n_half)
-            nc.tensor.matmul(
-                out=ln_b_bank[:],
-                lhsT=ident_bf16[:],
-                rhs=ln_b_rows[:, n_half * BANK : (n_half + 1) * BANK],
-                start=True,
-                stop=True,
-            )
-            ln_b_banks.append(ln_b_bank)
-
         def scale_and_store(i):
             result = stage2.tile([P, E_OUT], F32)
             for n_half in range(HALVES):
@@ -294,7 +277,7 @@ def tile_tnlattention_pb_kernel(tc, attn, gate_low, Wg2, Wo, ln_w, ln_b, out):
                     out=result[:, cols],
                     in0=centred_of[i][:, cols],
                     scalar=rstd_of[i][:, 0:1],
-                    in1=ln_b_banks[n_half][:],
+                    in1=ln_b_rows[:, cols],
                     op0=ALU.mult,
                     op1=ALU.add,
                 )

from contextlib import ExitStack

import concourse.mybir as mybir
from concourse.masks import make_identity

F32 = mybir.dt.float32
BF16 = mybir.dt.bfloat16
U32 = mybir.dt.uint32
U8 = mybir.dt.uint8
FP8X4 = mybir.dt.float8_e4m3fn_x4
ACT = mybir.ActivationFunctionType
ALU = mybir.AluOpType

P = 128
TOKENS = 2048
E = 1024
D_GATE = 128
E_OUT = 1024
LN_EPS = 1e-5

TILES = TOKENS // P
PAIRS = TILES // 2
PAIR_TOKENS = 2 * P
PACK = 4
PASSES = E // (P * PACK)
UNITS = PAIRS * PASSES
BANK = 512
HALVES = E_OUT // BANK
WO_CHUNK = 128
WO_CHUNKS_PER_PASS = E_OUT // WO_CHUNK
WO_CHUNKS = PASSES * WO_CHUNKS_PER_PASS
WO_FIRST_UNIT = 2

FLOPS = 2 * TOKENS * E * E_OUT + 2 * TOKENS * D_GATE * E


def tile_tnlattention_pb_kernel(tc, attn, gate_low, Wg2, Wo, ln_w, ln_b, out):
    nc = tc.nc
    attn_rows = attn.flatten_outer_dims().rearrange("(p i) e -> p (i e)", i=TILES)
    gate_low_rows = gate_low.flatten_outer_dims().rearrange("(p i) d -> p (i d)", i=TILES)
    out_rows = out.flatten_outer_dims().rearrange("(p i) n -> p (i n)", i=TILES)

    with ExitStack() as stack:
        keep = stack.enter_context(tc.tile_pool(name="keep", bufs=1))
        stage1 = stack.enter_context(tc.tile_pool(name="stage1", bufs=3))
        stage2 = stack.enter_context(tc.tile_pool(name="stage2", bufs=4))
        psum = stack.enter_context(tc.psum_pool(name="psum", bufs=6))

        wg2_sb = keep.tile([P, E], BF16)
        gate_low_sb = keep.tile([P, TILES * D_GATE], BF16)
        attn_sb = keep.tile([P, TILES * E], BF16)
        wo_raw = keep.tile([P, PASSES, PACK, E_OUT], BF16)
        for pair in range(PAIRS):
            gate_cols = slice(pair * 2 * D_GATE, (pair + 1) * 2 * D_GATE)
            nc.sync.dma_start(out=gate_low_sb[:, gate_cols], in_=gate_low_rows[:, gate_cols])
            if pair == 0:
                nc.sync.dma_start(out=wg2_sb[:], in_=Wg2)
            attn_cols = slice(pair * 2 * E, (pair + 1) * 2 * E)
            nc.sync.dma_start(out=attn_sb[:, attn_cols], in_=attn_rows[:, attn_cols])
            if 1 <= pair <= PASSES:
                g = pair - 1
                nc.sync.dma_start(
                    out=wo_raw[:, g].rearrange("p (u e) n -> p u e n", e=2),
                    in_=Wo[g * P * PACK : (g + 1) * P * PACK, :].rearrange(
                        "(u p e) n -> p u e n", u=2, e=2
                    ),
                )
        ln_w_rows = keep.tile([P, E_OUT], BF16)
        nc.sync.dma_start(out=ln_w_rows[:], in_=ln_w.partition_broadcast(P))
        ln_b_rows = keep.tile([P, E_OUT], BF16)
        nc.sync.dma_start(out=ln_b_rows[:], in_=ln_b.partition_broadcast(P))

        ident_bf16 = keep.tile([P, P], BF16)
        make_identity(nc, ident_bf16[:])
        ident_f32 = keep.tile([P, P], F32)
        make_identity(nc, ident_f32[:])
        minus_half = keep.tile([P, 1], F32)
        nc.gpsimd.memset(minus_half[:], -0.5)

        table_in = keep.tile([P, 1], F32)
        nc.vector.memset(table_in[:], 0.0)
        table_out = keep.tile([P, 1], F32)
        nc.scalar.activation(out=table_out[:], in_=table_in[:], func=ACT.Sigmoid)

        wg2_by_word = wg2_sb[:].rearrange("d (a p e) -> d a e p", a=PASSES * 2, e=2)
        attn_words = attn_sb[:].bitcast(F32)

        wo_grouped = keep.tile([P, PASSES, E_OUT, PACK], BF16, align_bytes=64)
        wo_codes = keep.tile([P, PASSES, E_OUT], U32, align_bytes=64)
        wo_scales = keep.tile([P, PASSES, E_OUT], U8, align_bytes=64)
        h_codes = keep.tile([P, PAIRS, PASSES, PAIR_TOKENS], U32, align_bytes=64)
        h_scales = keep.tile([P, PAIRS, PASSES, PAIR_TOKENS], U8, align_bytes=64)
        gate_lowT = keep.tile([P, TILES * P], BF16)

        def wo_chunk(chunk):
            g, quarter = divmod(chunk, WO_CHUNKS_PER_PASS)
            return g, slice(quarter * WO_CHUNK, (quarter + 1) * WO_CHUNK)

        def regroup_wo(chunk):
            g, cols = wo_chunk(chunk)
            grouped = wo_grouped[:, g, cols, :].rearrange("p (c i) t -> p c t i", i=4)
            raw = wo_raw[:, g, :, cols].rearrange("p t (c i) -> p c t i", i=4)
            nc.scalar.copy(out=grouped, in_=raw)

        def quantise_wo(chunk):
            g, cols = wo_chunk(chunk)
            nc.vector.quantize_mx(
                out=wo_codes[:, g, cols].bitcast(FP8X4),
                scales=wo_scales[:, g, cols],
                in_=wo_grouped[:, g, cols, :].rearrange("p n t -> p (n t)"),
            )

        def turn_gate_low(pair):
            turned = psum.tile([P, PAIR_TOKENS], BF16, tag="bank")
            for half in range(2):
                i = 2 * pair + half
                nc.tensor.transpose(
                    out=turned[:, half * P : (half + 1) * P],
                    in_=gate_low_sb[:, i * D_GATE : (i + 1) * D_GATE],
                    identity=ident_bf16[:],
                )
            nc.vector.tensor_copy(
                out=gate_lowT[:, pair * PAIR_TOKENS : (pair + 1) * PAIR_TOKENS], in_=turned[:]
            )

        def gated_unit(pair, g, h_grouped):
            sig = stage1.tile([P, PAIR_TOKENS, PACK], F32)
            for half in range(2):
                i = 2 * pair + half
                gateT = psum.tile([P, PACK, P], F32, tag="bank")
                for t in range(PACK):
                    u, e = divmod(t, 2)
                    nc.tensor.matmul(
                        out=gateT[:, t, :],
                        lhsT=wg2_by_word[:, 2 * g + u, e, :],
                        rhs=gate_lowT[:, i * P : (i + 1) * P],
                        start=True,
                        stop=True,
                    )
                nc.scalar.activation(
                    out=sig[:, half * P : (half + 1) * P, :],
                    in_=gateT[:].rearrange("p t m -> p m t"),
                    func=ACT.Sigmoid,
                )
            attnT = psum.tile([P, BANK], F32, tag="bank")
            for u in range(2):
                for half in range(2):
                    word0 = (2 * pair + half) * (E // 2) + (2 * g + u) * P
                    nc.tensor.transpose(
                        out=attnT[:, (2 * u + half) * P : (2 * u + half + 1) * P],
                        in_=attn_words[:, word0 : word0 + P],
                        identity=ident_f32[:],
                    )
            nc.vector.tensor_tensor(
                out=h_grouped[:, g].rearrange("p m (u e) -> p m u e", e=2),
                in0=attnT[:].bitcast(BF16).rearrange("p (u m e) -> p m u e", u=2, e=2),
                in1=sig[:].rearrange("p m (u e) -> p m u e", e=2),
                op=ALU.mult,
            )

        def quantise_h(pair, h_grouped):
            nc.vector.quantize_mx(
                out=h_codes[:, pair].rearrange("p g m -> p (g m)").bitcast(FP8X4),
                scales=h_scales[:, pair].rearrange("p g m -> p (g m)"),
                in_=h_grouped[:].rearrange("p g m t -> p (g m t)"),
            )

        h_grouped_of = {}
        turn_gate_low(0)
        for step in range(UNITS + WO_FIRST_UNIT + 1):
            pair, g = divmod(step, PASSES)
            if step < UNITS:
                if g == 0:
                    h_grouped = stage1.tile([P, PASSES, PAIR_TOKENS, PACK], BF16, align_bytes=64)
                    h_grouped_of[pair] = h_grouped
                if g == PASSES - 1 and pair + 1 < PAIRS:
                    turn_gate_low(pair + 1)
                gated_unit(pair, g, h_grouped_of[pair])
            chunk = step - WO_FIRST_UNIT
            if 0 <= chunk < WO_CHUNKS:
                regroup_wo(chunk)
            if 0 <= chunk - 1 < WO_CHUNKS:
                quantise_wo(chunk - 1)
            if g == 0 and 1 <= pair <= PAIRS:
                quantise_h(pair - 1, h_grouped_of[pair - 1])

        y_of = {}
        y_copy_of = {}
        neg_mean_of = {}
        rstd_of = {}
        centred_of = {}

        def project(i):
            pair, half = divmod(i, 2)
            tokens = slice(half * P, (half + 1) * P)
            banks = []
            for n_half in range(HALVES):
                cols = slice(n_half * BANK, (n_half + 1) * BANK)
                y = psum.tile([P, BANK], F32, tag="bank")
                for g in range(PASSES):
                    nc.tensor.matmul_mx(
                        out=y[:],
                        lhsT=h_codes[:, pair, g, tokens].bitcast(FP8X4),
                        lhsT_scale=h_scales[:, pair, g, tokens],
                        rhs=wo_codes[:, g, cols].bitcast(FP8X4),
                        rhs_scale=wo_scales[:, g, cols],
                        start=(g == 0),
                        stop=(g == PASSES - 1),
                    )
                banks.append(y)
            y_of[i] = banks

        def row_means(i):
            y_copy = stage2.tile([P, E_OUT], F32)
            sums = stage2.tile([P, HALVES], F32)
            for n_half in range(HALVES):
                nc.scalar.activation(
                    out=y_copy[:, n_half * BANK : (n_half + 1) * BANK],
                    in_=y_of[i][n_half][:],
                    func=ACT.Identity,
                    accum_out=sums[:, n_half : n_half + 1],
                )
            neg_mean = stage2.tile([P, 1], F32)
            nc.gpsimd.tensor_scalar(
                out=neg_mean[:],
                in0=sums[:, 0:1],
                scalar1=sums[:, 1:2],
                scalar2=-1.0 / E_OUT,
                op0=ALU.add,
                op1=ALU.mult,
            )
            y_copy_of[i] = y_copy
            neg_mean_of[i] = neg_mean

        def row_rstds(i):
            squares = stage2.tile([P, E_OUT], BF16)
            square_sum = stage2.tile([P, 1], F32)
            nc.scalar.activation(
                out=squares[:],
                in_=y_copy_of[i][:],
                func=ACT.Square,
                bias=neg_mean_of[i][:, 0:1],
                accum_out=square_sum[:],
            )
            var_eps = stage2.tile([P, 1], F32)
            nc.gpsimd.tensor_scalar(
                out=var_eps[:],
                in0=square_sum[:],
                scalar1=1.0 / E_OUT,
                scalar2=LN_EPS,
                op0=ALU.mult,
                op1=ALU.add,
            )
            rstd = stage2.tile([P, 1], F32)
            nc.gpsimd.tensor_tensor(out=rstd[:], in0=var_eps[:], in1=minus_half[:], op=ALU.pow)
            rstd_of[i] = rstd

        def centre(i):
            centred = stage2.tile([P, E_OUT], F32)
            for n_half in range(HALVES):
                cols = slice(n_half * BANK, (n_half + 1) * BANK)
                nc.vector.scalar_tensor_tensor(
                    out=centred[:, cols],
                    in0=y_of[i][n_half][:],
                    scalar=neg_mean_of[i][:, 0:1],
                    in1=ln_w_rows[:, cols],
                    op0=ALU.add,
                    op1=ALU.mult,
                )
            centred_of[i] = centred

        def scale_and_store(i):
            result = stage2.tile([P, E_OUT], F32)
            for n_half in range(HALVES):
                cols = slice(n_half * BANK, (n_half + 1) * BANK)
                nc.vector.scalar_tensor_tensor(
                    out=result[:, cols],
                    in0=centred_of[i][:, cols],
                    scalar=rstd_of[i][:, 0:1],
                    in1=ln_b_rows[:, cols],
                    op0=ALU.mult,
                    op1=ALU.add,
                )
                nc.sync.dma_start(
                    out=out_rows[:, i * E_OUT + n_half * BANK : i * E_OUT + (n_half + 1) * BANK],
                    in_=result[:, cols],
                )

        for step in range(TILES + 2):
            if step < TILES:
                project(step)
                row_means(step)
            if 1 <= step <= TILES:
                row_rstds(step - 1)
                centre(step - 1)
            if step >= 2:
                scale_and_store(step - 2)
